import numpy as np
import ml_dtypes


def mxq(x, axis, fmt="e4m3"):
    dtype, down = {"e4m3": (ml_dtypes.float8_e4m3fn, 7), "e5m2": (ml_dtypes.float8_e5m2, 14)}[fmt]
    v = np.moveaxis(np.asarray(x, np.float32).astype(ml_dtypes.bfloat16).astype(np.float64), axis, -1)
    blocks = v.reshape(v.shape[:-1] + (-1, 32))
    amax = np.abs(blocks).max(-1, keepdims=True)
    byte = np.maximum(np.where(amax > 0, np.frexp(amax)[1] - 1 + 127, 0) - down, 1)
    scale = np.exp2(byte - 127.0)
    codes = (blocks / scale).astype(np.float32).astype(dtype).astype(np.float64)
    return np.moveaxis((codes * scale).reshape(v.shape), -1, axis)


WIDE = False


def mx_kscale(k):
    if not WIDE:
        return np.ones(k)
    levels = np.array([10, -10, 5, -5, 0])
    a = np.random.permutation(np.resize(levels, k // 512 * 4)).reshape(k // 512, 4)
    idx = np.arange(k)
    return np.exp2(a[idx // 512, idx % 128 // 32])


BF16 = ml_dtypes.bfloat16


def bf(x):
    return np.asarray(x, np.float32).astype(BF16)


def f64(x):
    return np.asarray(x).astype(np.float64)


E2M1 = np.array([0.0, 0.5, 1.0, 1.5, 2.0, 3.0, 4.0, 6.0, -0.0, -0.5, -1.0, -1.5, -2.0, -3.0, -4.0, -6.0])


def pack_weight(w, fmt):
    k, n = w.shape
    w = f64(bf(w)).reshape(k // 32, 32, n)
    amax = np.abs(w).max(1)
    if fmt == "e4m3":
        byte = np.frexp(amax)[1] - 1 + 127 - 7
    else:
        mant, ex = np.frexp(amax / 6.0)
        byte = np.where(mant > 0.5, ex, ex - 1) + 127
    byte = np.clip(np.where(amax > 0, byte, 1), 1, 254)
    scaled = (w * np.exp2(127.0 - byte)[:, None, :]).reshape(k, n).astype(np.float32)
    by_word = np.ascontiguousarray(scaled.reshape(k // 512, 128, 4, n).transpose(0, 1, 3, 2))
    if fmt == "e4m3":
        words = by_word.astype(ml_dtypes.float8_e4m3fn).view(np.uint8)
    else:
        c = by_word.astype(ml_dtypes.float4_e2m1fn).view(np.uint8) & 0xF
        words = c[..., 0::2] | (c[..., 1::2] << 4)
    return np.ascontiguousarray(words), np.ascontiguousarray(byte.astype(np.uint8).reshape(k // 512, 16, n))


def unpack_weight(words, scales, fmt):
    g, p, n, _ = words.shape
    if fmt == "e4m3":
        vals = np.ascontiguousarray(words).view(ml_dtypes.float8_e4m3fn).astype(np.float64)
    else:
        nib = np.empty((g, p, n, 4), np.uint8)
        nib[..., 0::2] = words & 0xF
        nib[..., 1::2] = words >> 4
        vals = E2M1[nib]
    vals = vals * np.repeat(np.exp2(scales.astype(np.float64) - 127.0), 8, axis=1)[..., None]
    return vals.transpose(0, 1, 3, 2).reshape(g * 512, n)


N, I, O = 512, 2048, 2048
FMT = "e4m3"


def setup_inputs():
    s = mx_kscale(I)
    mask = np.tile(np.array([0.0, 0.0, 1.0, 1.0]), I // 4)
    gd = mask + 0.1 * (1.0 - mask)
    gs = (1.0 - mask) + 0.1 * mask
    x = np.random.standard_normal((N, I)) * s
    wd = np.random.standard_normal((O, I)) * gd / np.sqrt(I) / s
    ws = np.random.standard_normal((O, I)) * gs / np.sqrt(I) / s
    wd_words, wd_scales = pack_weight(np.ascontiguousarray(wd.T), FMT)
    ws_words, ws_scales = pack_weight(np.ascontiguousarray(ws.T), FMT)
    return {"x": bf(x), "W_dense_words": wd_words, "W_dense_scales": wd_scales, "W_sparse_words": ws_words, "W_sparse_scales": ws_scales}


def reference(x, W_dense_words, W_dense_scales, W_sparse_words, W_sparse_scales):
    xq = mxq(f64(x), 1, "e4m3")
    out_dense = xq @ unpack_weight(W_dense_words, W_dense_scales, FMT)
    out_sparse = xq @ unpack_weight(W_sparse_words, W_sparse_scales, FMT)
    return out_dense + out_sparse

@@ -1,0 +1,151 @@
+from contextlib import ExitStack
+
+import concourse.mybir as mybir
+from concourse.masks import make_identity
+
+F32 = mybir.dt.float32
+BF16 = mybir.dt.bfloat16
+I32 = mybir.dt.int32
+U32 = mybir.dt.uint32
+U8 = mybir.dt.uint8
+FP8X4 = mybir.dt.float8_e4m3fn_x4
+
+P = 128
+PACK = 4
+K_PASS = P * PACK
+TOKENS = 512
+K = 2048
+N = 2048
+PASSES = K // K_PASS
+TOKEN_TILES = TOKENS // P
+N_TILE = 512
+N_TILES = N // N_TILE
+WEIGHTS = 2
+BANKS = 8
+BANK_F32 = 512
+PAIRS = 2
+PASS_WORDS = K_PASS // 2
+PASSES_PER_BANK = BANK_F32 // (PAIRS * P)
+QUADRANTS = 4
+
+FLOPS = 2 * WEIGHTS * TOKENS * K * N
+
+
+def tile_myinterleavedmodule_kernel(
+    tc, x, W_dense_words, W_dense_scales, W_sparse_words, W_sparse_scales, out
+):
+    nc = tc.nc
+    w_words_dram = [W_dense_words, W_sparse_words]
+    w_scales_dram = [W_dense_scales, W_sparse_scales]
+
+    with ExitStack() as ctx:
+        ctx.enter_context(tc.manual_schedule())
+        keep = ctx.enter_context(tc.tile_pool(name="keep", bufs=1))
+        stage = ctx.enter_context(tc.tile_pool(name="stage", bufs=4))
+        results = ctx.enter_context(tc.tile_pool(name="results", bufs=TOKEN_TILES * N_TILES))
+        psum = ctx.enter_context(tc.psum_pool(name="psum", bufs=BANKS))
+
+        ident = keep.tile([P, P], F32, name="ident")
+        x_sb = [keep.tile([P, K], BF16, name="x_sb%d" % i) for i in range(TOKEN_TILES)]
+        x_codes = [
+            keep.tile([P, PASSES * P], U32, name="x_codes%d" % i, align_bytes=64)
+            for i in range(TOKEN_TILES)
+        ]
+        x_scales = [
+            keep.tile([P, PASSES * P], U8, name="x_scales%d" % i, align_bytes=64)
+            for i in range(TOKEN_TILES)
+        ]
+        w_chunk = {}
+        for w in range(WEIGHTS):
+            for g in range(PASSES):
+                for j in range(N_TILES):
+                    w_chunk[(w, g, j)] = keep.tile(
+                        [P, N_TILE], U32, name="w%d_g%d_j%d" % (w, g, j), align_bytes=64
+                    )
+        w_scales = [keep.tile([P, N], U8, name="w_scales%d" % w, align_bytes=64) for w in range(WEIGHTS)]
+
+        for w in range(WEIGHTS):
+            nc.vector.memset(w_scales[w][:].bitcast(I32), 0)
+        make_identity(nc, ident[:])
+
+        def load_scales(w):
+            for q in range(QUADRANTS):
+                nc.sync.dma_start(
+                    out=w_scales[w][32 * q : 32 * q + 16, :].bitcast(I32),
+                    in_=w_scales_dram[w][:, 4 * q : 4 * q + 4, :].bitcast(I32),
+                )
+
+        def load_chunk(w, g, j):
+            words = w_words_dram[w][g].rearrange("p n t -> p (n t)")
+            nc.sync.dma_start(
+                out=w_chunk[(w, g, j)][:].bitcast(I32),
+                in_=words[:, PACK * N_TILE * j : PACK * N_TILE * (j + 1)].bitcast(I32),
+            )
+
+        for i in range(TOKEN_TILES):
+            nc.sync.dma_start(out=x_sb[i][:], in_=x[P * i : P * (i + 1), :])
+        for j in range(N_TILES):
+            for w in range(WEIGHTS):
+                if j == 0:
+                    load_scales(w)
+                for g in range(PASSES):
+                    load_chunk(w, g, j)
+
+        for i in range(TOKEN_TILES):
+            x_pairs = x_sb[i][:].bitcast(F32)
+            for h in range(PASSES // PASSES_PER_BANK):
+                flipped = psum.tile([P, BANK_F32], F32, tag="bank", name="flipped")
+                for s in range(PASSES_PER_BANK):
+                    g = PASSES_PER_BANK * h + s
+                    for u in range(PAIRS):
+                        block = PAIRS * s + u
+                        nc.tensor.transpose(
+                            flipped[:, P * block : P * (block + 1)],
+                            x_pairs[:, PASS_WORDS * g + u : PASS_WORDS * (g + 1) : PAIRS],
+                            ident[:],
+                        )
+                grouped = stage.tile([P, PASSES_PER_BANK * P * PACK], BF16, name="grouped", align_bytes=64)
+                nc.scalar.copy(
+                    out=grouped[:].bitcast(F32).rearrange("p (s r u) -> p s r u", s=PASSES_PER_BANK, u=PAIRS),
+                    in_=flipped[:].rearrange("p (s u r) -> p s r u", s=PASSES_PER_BANK, u=PAIRS),
+                )
+                cols = slice(PASSES_PER_BANK * P * h, PASSES_PER_BANK * P * (h + 1))
+                nc.vector.quantize_mx(
+                    out=x_codes[i][:, cols].bitcast(FP8X4),
+                    scales=x_scales[i][:, cols],
+                    in_=grouped[:],
+                )
+
+        def mx_pass(acc, i, w, g, j):
+            nc.tensor.matmul_mx(
+                out=acc[:],
+                lhsT=x_codes[i][:, P * g : P * (g + 1)].bitcast(FP8X4),
+                lhsT_scale=x_scales[i][:, P * g : P * (g + 1)],
+                rhs=w_chunk[(w, g, j)][:].bitcast(FP8X4),
+                rhs_scale=w_scales[w][4 * g : P, N_TILE * j : N_TILE * (j + 1)],
+                start=(w == 0 and g == 0),
+                stop=(w == WEIGHTS - 1 and g == PASSES - 1),
+            )
+
+        def store(acc, i, j):
+            result = results.tile([P, N_TILE], F32, name="result")
+            if i % 2 == 0:
+                nc.vector.tensor_copy(out=result[:], in_=acc[:])
+            else:
+                nc.scalar.copy(out=result[:], in_=acc[:])
+            nc.sync.dma_start(out=out[P * i : P * (i + 1), N_TILE * j : N_TILE * (j + 1)], in_=result[:])
+
+        for j in range(N_TILES):
+            accs = [psum.tile([P, N_TILE], F32, tag="bank", name="acc%d" % i) for i in range(TOKEN_TILES)]
+            if j < N_TILES - 1:
+                for w in range(WEIGHTS):
+                    for g in range(PASSES):
+                        for i in range(TOKEN_TILES):
+                            mx_pass(accs[i], i, w, g, j)
+            else:
+                for i in range(TOKEN_TILES):
+                    for w in range(WEIGHTS):
+                        for g in range(PASSES):
+                            mx_pass(accs[i], i, w, g, j)
+            for i in range(TOKEN_TILES):
+                store(accs[i], i, j)

@@ -68,12 +68,18 @@ def tile_myinterleavedmodule_kernel(
             nc.vector.memset(w_scales[w][:].bitcast(I32), 0)
         make_identity(nc, ident[:])
 
-        def load_scales(w):
+        for i in range(TOKEN_TILES):
+            nc.sync.dma_start(out=x_sb[i][:], in_=x[P * i : P * (i + 1), :])
+
+        def load_scales(w, queue):
             for q in range(QUADRANTS):
-                nc.sync.dma_start(
-                    out=w_scales[w][32 * q : 32 * q + 16, :].bitcast(I32),
-                    in_=w_scales_dram[w][:, 4 * q : 4 * q + 4, :].bitcast(I32),
+                queue.dma_start(
+                    out=w_scales[w][32 * q : 32 * q + 16, :].bitcast(F32),
+                    in_=w_scales_dram[w][:, 4 * q : 4 * q + 4, :].bitcast(F32),
                 )
+
+        load_scales(0, nc.scalar)
+        load_scales(1, nc.gpsimd)
 
         def load_chunk(w, g, j):
             words = w_words_dram[w][g].rearrange("p n t -> p (n t)")
@@ -82,12 +88,8 @@ def tile_myinterleavedmodule_kernel(
                 in_=words[:, PACK * N_TILE * j : PACK * N_TILE * (j + 1)].bitcast(I32),
             )
 
-        for i in range(TOKEN_TILES):
-            nc.sync.dma_start(out=x_sb[i][:], in_=x[P * i : P * (i + 1), :])
         for j in range(N_TILES):
             for w in range(WEIGHTS):
-                if j == 0:
-                    load_scales(w)
                 for g in range(PASSES):
                     load_chunk(w, g, j)
 
@@ -105,7 +107,9 @@ def tile_myinterleavedmodule_kernel(
                             ident[:],
                         )
                 grouped = stage.tile([P, PASSES_PER_BANK * P * PACK], BF16, name="grouped", align_bytes=64)
-                nc.scalar.copy(
+                bank = (PASSES // PASSES_PER_BANK) * i + h
+                copy_out = nc.vector.tensor_copy if bank % 4 == 3 else nc.scalar.copy
+                copy_out(
                     out=grouped[:].bitcast(F32).rearrange("p (s r u) -> p s r u", s=PASSES_PER_BANK, u=PAIRS),
                     in_=flipped[:].rearrange("p (s u r) -> p s r u", s=PASSES_PER_BANK, u=PAIRS),
                 )

@@ -20,6 +20,7 @@ PASSES = K // K_PASS
 TOKEN_TILES = TOKENS // P
 N_TILE = 512
 N_TILES = N // N_TILE
+LAST_N = 256
 WEIGHTS = 2
 BANKS = 8
 BANK_F32 = 512
@@ -27,6 +28,7 @@ PAIRS = 2
 PASS_WORDS = K_PASS // 2
 PASSES_PER_BANK = BANK_F32 // (PAIRS * P)
 QUADRANTS = 4
+PIECES = TOKEN_TILES * (N_TILES - 1 + N_TILE // LAST_N)
 
 FLOPS = 2 * WEIGHTS * TOKENS * K * N
 
@@ -42,7 +44,7 @@ def tile_myinterleavedmodule_kernel(
         ctx.enter_context(tc.manual_schedule())
         keep = ctx.enter_context(tc.tile_pool(name="keep", bufs=1))
         stage = ctx.enter_context(tc.tile_pool(name="stage", bufs=4))
-        results = ctx.enter_context(tc.tile_pool(name="results", bufs=TOKEN_TILES * N_TILES))
+        results = ctx.enter_context(tc.tile_pool(name="results", bufs=PIECES))
         psum = ctx.enter_context(tc.psum_pool(name="psum", bufs=BANKS))
 
         ident = keep.tile([P, P], F32, name="ident")
@@ -68,18 +70,12 @@ def tile_myinterleavedmodule_kernel(
             nc.vector.memset(w_scales[w][:].bitcast(I32), 0)
         make_identity(nc, ident[:])
 
-        for i in range(TOKEN_TILES):
-            nc.sync.dma_start(out=x_sb[i][:], in_=x[P * i : P * (i + 1), :])
-
-        def load_scales(w, queue):
+        def load_scales(w):
             for q in range(QUADRANTS):
-                queue.dma_start(
-                    out=w_scales[w][32 * q : 32 * q + 16, :].bitcast(F32),
-                    in_=w_scales_dram[w][:, 4 * q : 4 * q + 4, :].bitcast(F32),
+                nc.sync.dma_start(
+                    out=w_scales[w][32 * q : 32 * q + 16, :].bitcast(I32),
+                    in_=w_scales_dram[w][:, 4 * q : 4 * q + 4, :].bitcast(I32),
                 )
-
-        load_scales(0, nc.scalar)
-        load_scales(1, nc.gpsimd)
 
         def load_chunk(w, g, j):
             words = w_words_dram[w][g].rearrange("p n t -> p (n t)")
@@ -88,8 +84,12 @@ def tile_myinterleavedmodule_kernel(
                 in_=words[:, PACK * N_TILE * j : PACK * N_TILE * (j + 1)].bitcast(I32),
             )
 
+        for i in range(TOKEN_TILES):
+            nc.sync.dma_start(out=x_sb[i][:], in_=x[P * i : P * (i + 1), :])
         for j in range(N_TILES):
             for w in range(WEIGHTS):
+                if j == 0:
+                    load_scales(w)
                 for g in range(PASSES):
                     load_chunk(w, g, j)
 
@@ -107,9 +107,7 @@ def tile_myinterleavedmodule_kernel(
                             ident[:],
                         )
                 grouped = stage.tile([P, PASSES_PER_BANK * P * PACK], BF16, name="grouped", align_bytes=64)
-                bank = (PASSES // PASSES_PER_BANK) * i + h
-                copy_out = nc.vector.tensor_copy if bank % 4 == 3 else nc.scalar.copy
-                copy_out(
+                nc.scalar.copy(
                     out=grouped[:].bitcast(F32).rearrange("p (s r u) -> p s r u", s=PASSES_PER_BANK, u=PAIRS),
                     in_=flipped[:].rearrange("p (s u r) -> p s r u", s=PASSES_PER_BANK, u=PAIRS),
                 )
@@ -120,36 +118,42 @@ def tile_myinterleavedmodule_kernel(
                     in_=grouped[:],
                 )
 
-        def mx_pass(acc, i, w, g, j):
+        def mx_pass(acc, i, w, g, n0, width):
+            j = n0 // N_TILE
+            first = n0 % N_TILE
             nc.tensor.matmul_mx(
                 out=acc[:],
                 lhsT=x_codes[i][:, P * g : P * (g + 1)].bitcast(FP8X4),
                 lhsT_scale=x_scales[i][:, P * g : P * (g + 1)],
-                rhs=w_chunk[(w, g, j)][:].bitcast(FP8X4),
-                rhs_scale=w_scales[w][4 * g : P, N_TILE * j : N_TILE * (j + 1)],
+                rhs=w_chunk[(w, g, j)][:, first : first + width].bitcast(FP8X4),
+                rhs_scale=w_scales[w][4 * g : P, n0 : n0 + width],
                 start=(w == 0 and g == 0),
                 stop=(w == WEIGHTS - 1 and g == PASSES - 1),
             )
 
-        def store(acc, i, j):
-            result = results.tile([P, N_TILE], F32, name="result")
-            if i % 2 == 0:
-                nc.vector.tensor_copy(out=result[:], in_=acc[:])
-            else:
+        def store(acc, piece, i, n0, width):
+            result = results.tile([P, width], F32, name="result")
+            if piece % 2 == 0:
                 nc.scalar.copy(out=result[:], in_=acc[:])
-            nc.sync.dma_start(out=out[P * i : P * (i + 1), N_TILE * j : N_TILE * (j + 1)], in_=result[:])
+            else:
+                nc.vector.tensor_copy(out=result[:], in_=acc[:])
+            nc.sync.dma_start(out=out[P * i : P * (i + 1), n0 : n0 + width], in_=result[:])
 
-        for j in range(N_TILES):
+        for j in range(N_TILES - 1):
             accs = [psum.tile([P, N_TILE], F32, tag="bank", name="acc%d" % i) for i in range(TOKEN_TILES)]
-            if j < N_TILES - 1:
+            for w in range(WEIGHTS):
+                for g in range(PASSES):
+                    for i in range(TOKEN_TILES):
+                        mx_pass(accs[i], i, w, g, N_TILE * j, N_TILE)
+            for i in range(TOKEN_TILES):
+                store(accs[i], i, i, N_TILE * j, N_TILE)
+
+        halves = N_TILE // LAST_N
+        for i in range(TOKEN_TILES):
+            for half in range(halves):
+                n0 = N_TILE * (N_TILES - 1) + LAST_N * half
+                acc = psum.tile([P, LAST_N], F32, tag="bank", name="acc_last")
                 for w in range(WEIGHTS):
                     for g in range(PASSES):
-                        for i in range(TOKEN_TILES):
-                            mx_pass(accs[i], i, w, g, j)
-            else:
-                for i in range(TOKEN_TILES):
-                    for w in range(WEIGHTS):
-                        for g in range(PASSES):
-                            mx_pass(accs[i], i, w, g, j)
-            for i in range(TOKEN_TILES):
-                store(accs[i], i, j)
+                        mx_pass(acc, i, w, g, n0, LAST_N)
+                store(acc, halves * i + half, i, n0, LAST_N)

@@ -22,13 +22,15 @@ N_TILE = 512
 N_TILES = N // N_TILE
 LAST_N = 256
 WEIGHTS = 2
-BANKS = 8
 BANK_F32 = 512
 PAIRS = 2
 PASS_WORDS = K_PASS // 2
 PASSES_PER_BANK = BANK_F32 // (PAIRS * P)
+HALVES = PASSES // PASSES_PER_BANK
 QUADRANTS = 4
 PIECES = TOKEN_TILES * (N_TILES - 1 + N_TILE // LAST_N)
+WARM_FIRST = 5
+WARM_BETWEEN = 2
 
 FLOPS = 2 * WEIGHTS * TOKENS * K * N
 
@@ -45,10 +47,14 @@ def tile_myinterleavedmodule_kernel(
         keep = ctx.enter_context(tc.tile_pool(name="keep", bufs=1))
         stage = ctx.enter_context(tc.tile_pool(name="stage", bufs=4))
         results = ctx.enter_context(tc.tile_pool(name="results", bufs=PIECES))
-        psum = ctx.enter_context(tc.psum_pool(name="psum", bufs=BANKS))
+        psum = ctx.enter_context(tc.psum_pool(name="psum", bufs=4))
 
         ident = keep.tile([P, P], F32, name="ident")
-        x_sb = [keep.tile([P, K], BF16, name="x_sb%d" % i) for i in range(TOKEN_TILES)]
+        zeros = keep.tile([P, N_TILE], BF16, name="zeros")
+        x_sb = {}
+        for i in range(TOKEN_TILES):
+            for h in range(HALVES):
+                x_sb[(i, h)] = keep.tile([P, K // HALVES], BF16, name="x_sb%d_%d" % (i, h))
         x_codes = [
             keep.tile([P, PASSES * P], U32, name="x_codes%d" % i, align_bytes=64)
             for i in range(TOKEN_TILES)
@@ -66,15 +72,20 @@ def tile_myinterleavedmodule_kernel(
                     )
         w_scales = [keep.tile([P, N], U8, name="w_scales%d" % w, align_bytes=64) for w in range(WEIGHTS)]
 
+        nc.vector.memset(zeros[:], 0.0)
         for w in range(WEIGHTS):
             nc.vector.memset(w_scales[w][:].bitcast(I32), 0)
         make_identity(nc, ident[:])
 
-        def load_scales(w):
+        def load_x(i, h):
+            width = K // HALVES
+            nc.sync.dma_start(out=x_sb[(i, h)][:], in_=x[P * i : P * (i + 1), width * h : width * (h + 1)])
+
+        def load_scales(w, n0, n1):
             for q in range(QUADRANTS):
                 nc.sync.dma_start(
-                    out=w_scales[w][32 * q : 32 * q + 16, :].bitcast(I32),
-                    in_=w_scales_dram[w][:, 4 * q : 4 * q + 4, :].bitcast(I32),
+                    out=w_scales[w][32 * q : 32 * q + 16, n0:n1].bitcast(I32),
+                    in_=w_scales_dram[w][:, 4 * q : 4 * q + 4, n0:n1].bitcast(I32),
                 )
 
         def load_chunk(w, g, j):
@@ -85,50 +96,62 @@ def tile_myinterleavedmodule_kernel(
             )
 
         for i in range(TOKEN_TILES):
-            nc.sync.dma_start(out=x_sb[i][:], in_=x[P * i : P * (i + 1), :])
-        for j in range(N_TILES):
+            load_x(i, 0)
+        for w in range(WEIGHTS):
+            load_scales(w, 0, N_TILE)
+        for g in range(PASSES):
             for w in range(WEIGHTS):
-                if j == 0:
-                    load_scales(w)
+                load_chunk(w, g, 0)
+            if g == 0:
+                for i in range(TOKEN_TILES):
+                    load_x(i, 1)
+        for w in range(WEIGHTS):
+            load_scales(w, N_TILE, N)
+        for j in range(1, N_TILES):
+            for w in range(WEIGHTS):
                 for g in range(PASSES):
                     load_chunk(w, g, j)
 
-        for i in range(TOKEN_TILES):
-            x_pairs = x_sb[i][:].bitcast(F32)
-            for h in range(PASSES // PASSES_PER_BANK):
-                flipped = psum.tile([P, BANK_F32], F32, tag="bank", name="flipped")
-                for s in range(PASSES_PER_BANK):
-                    g = PASSES_PER_BANK * h + s
-                    for u in range(PAIRS):
-                        block = PAIRS * s + u
-                        nc.tensor.transpose(
-                            flipped[:, P * block : P * (block + 1)],
-                            x_pairs[:, PASS_WORDS * g + u : PASS_WORDS * (g + 1) : PAIRS],
-                            ident[:],
-                        )
-                grouped = stage.tile([P, PASSES_PER_BANK * P * PACK], BF16, name="grouped", align_bytes=64)
-                nc.scalar.copy(
-                    out=grouped[:].bitcast(F32).rearrange("p (s r u) -> p s r u", s=PASSES_PER_BANK, u=PAIRS),
-                    in_=flipped[:].rearrange("p (s u r) -> p s r u", s=PASSES_PER_BANK, u=PAIRS),
-                )
-                cols = slice(PASSES_PER_BANK * P * h, PASSES_PER_BANK * P * (h + 1))
-                nc.vector.quantize_mx(
-                    out=x_codes[i][:, cols].bitcast(FP8X4),
-                    scales=x_scales[i][:, cols],
-                    in_=grouped[:],
-                )
+        idle_bank = psum.tile([P, N_TILE], F32, tag="B", name="idle_bank")
 
-        def mx_pass(acc, i, w, g, n0, width):
+        def warm(count):
+            for c in range(count):
+                nc.tensor.matmul(idle_bank[:], lhsT=zeros[:, 0:P], rhs=zeros[:], start=True, stop=True)
+
+        def flip(i, h):
+            x_pairs = x_sb[(i, h)][:].bitcast(F32)
+            flipped = psum.tile([P, BANK_F32], F32, tag="A", name="flipped")
+            for s in range(PASSES_PER_BANK):
+                for u in range(PAIRS):
+                    block = PAIRS * s + u
+                    nc.tensor.transpose(
+                        flipped[:, P * block : P * (block + 1)],
+                        x_pairs[:, PASS_WORDS * s + u : PASS_WORDS * (s + 1) : PAIRS],
+                        ident[:],
+                    )
+            grouped = stage.tile([P, PASSES_PER_BANK * P * PACK], BF16, name="grouped", align_bytes=64)
+            nc.scalar.copy(
+                out=grouped[:].bitcast(F32).rearrange("p (s r u) -> p s r u", s=PASSES_PER_BANK, u=PAIRS),
+                in_=flipped[:].rearrange("p (s u r) -> p s r u", s=PASSES_PER_BANK, u=PAIRS),
+            )
+            cols = slice(PASSES_PER_BANK * P * h, PASSES_PER_BANK * P * (h + 1))
+            nc.vector.quantize_mx(
+                out=x_codes[i][:, cols].bitcast(FP8X4),
+                scales=x_scales[i][:, cols],
+                in_=grouped[:],
+            )
+
+        def mx_pass(acc, i, w, g, n0, width, first, last):
             j = n0 // N_TILE
-            first = n0 % N_TILE
+            c0 = n0 % N_TILE
             nc.tensor.matmul_mx(
                 out=acc[:],
                 lhsT=x_codes[i][:, P * g : P * (g + 1)].bitcast(FP8X4),
                 lhsT_scale=x_scales[i][:, P * g : P * (g + 1)],
-                rhs=w_chunk[(w, g, j)][:, first : first + width].bitcast(FP8X4),
+                rhs=w_chunk[(w, g, j)][:, c0 : c0 + width].bitcast(FP8X4),
                 rhs_scale=w_scales[w][4 * g : P, n0 : n0 + width],
-                start=(w == 0 and g == 0),
-                stop=(w == WEIGHTS - 1 and g == PASSES - 1),
+                start=first,
+                stop=last,
             )
 
         def store(acc, piece, i, n0, width):
@@ -139,12 +162,31 @@ def tile_myinterleavedmodule_kernel(
                 nc.vector.tensor_copy(out=result[:], in_=acc[:])
             nc.sync.dma_start(out=out[P * i : P * (i + 1), n0 : n0 + width], in_=result[:])
 
-        for j in range(N_TILES - 1):
-            accs = [psum.tile([P, N_TILE], F32, tag="bank", name="acc%d" % i) for i in range(TOKEN_TILES)]
+        warm(WARM_FIRST)
+        for i in range(TOKEN_TILES):
+            flip(i, 0)
+            if i % 2 == 1:
+                warm(WARM_BETWEEN)
+
+        accs = [psum.tile([P, N_TILE], F32, tag="B", name="acc%d" % i) for i in range(TOKEN_TILES)]
+        for g in range(PASSES):
+            for w in range(WEIGHTS):
+                for i in range(TOKEN_TILES):
+                    mx_pass(accs[i], i, w, g, 0, N_TILE, g == 0 and w == 0, g == PASSES - 1 and w == WEIGHTS - 1)
+            if g == 0:
+                for i in range(TOKEN_TILES):
+                    flip(i, 1)
+        for i in range(TOKEN_TILES):
+            store(accs[i], i, i, 0, N_TILE)
+
+        for j in range(1, N_TILES - 1):
+            accs = [
+                psum.tile([P, N_TILE], F32, tag="AB"[(j + 1) % 2], name="acc%d" % i) for i in range(TOKEN_TILES)
+            ]
             for w in range(WEIGHTS):
                 for g in range(PASSES):
                     for i in range(TOKEN_TILES):
-                        mx_pass(accs[i], i, w, g, N_TILE * j, N_TILE)
+                        mx_pass(accs[i], i, w, g, N_TILE * j, N_TILE, w == 0 and g == 0, w == WEIGHTS - 1 and g == PASSES - 1)
             for i in range(TOKEN_TILES):
                 store(accs[i], i, i, N_TILE * j, N_TILE)
 
@@ -152,8 +194,9 @@ def tile_myinterleavedmodule_kernel(
         for i in range(TOKEN_TILES):
             for half in range(halves):
                 n0 = N_TILE * (N_TILES - 1) + LAST_N * half
-                acc = psum.tile([P, LAST_N], F32, tag="bank", name="acc_last")
+                piece = halves * i + half
+                acc = psum.tile([P, LAST_N], F32, tag="AB"[piece // 4], name="acc_last")
                 for w in range(WEIGHTS):
                     for g in range(PASSES):
-                        mx_pass(acc, i, w, g, n0, LAST_N)
-                store(acc, halves * i + half, i, n0, LAST_N)
+                        mx_pass(acc, i, w, g, n0, LAST_N, w == 0 and g == 0, w == WEIGHTS - 1 and g == PASSES - 1)
+                store(acc, piece, i, n0, LAST_N)

@@ -95,16 +95,15 @@ def tile_myinterleavedmodule_kernel(
                 in_=words[:, PACK * N_TILE * j : PACK * N_TILE * (j + 1)].bitcast(I32),
             )
 
-        for i in range(TOKEN_TILES):
-            load_x(i, 0)
         for w in range(WEIGHTS):
+            for i in range(TOKEN_TILES):
+                load_x(i, w)
             load_scales(w, 0, N_TILE)
-        for g in range(PASSES):
+            for g in range(PASSES_PER_BANK):
+                load_chunk(w, g, 0)
+        for g in range(PASSES_PER_BANK, PASSES):
             for w in range(WEIGHTS):
                 load_chunk(w, g, 0)
-            if g == 0:
-                for i in range(TOKEN_TILES):
-                    load_x(i, 1)
         for w in range(WEIGHTS):
             load_scales(w, N_TILE, N)
         for j in range(1, N_TILES):
@@ -169,13 +168,15 @@ def tile_myinterleavedmodule_kernel(
                 warm(WARM_BETWEEN)
 
         accs = [psum.tile([P, N_TILE], F32, tag="B", name="acc%d" % i) for i in range(TOKEN_TILES)]
-        for g in range(PASSES):
-            for w in range(WEIGHTS):
-                for i in range(TOKEN_TILES):
-                    mx_pass(accs[i], i, w, g, 0, N_TILE, g == 0 and w == 0, g == PASSES - 1 and w == WEIGHTS - 1)
-            if g == 0:
+        order = [(w, g) for w in range(WEIGHTS) for g in range(PASSES_PER_BANK)] + [
+            (w, g) for g in range(PASSES_PER_BANK, PASSES) for w in range(WEIGHTS)
+        ]
+        for step, (w, g) in enumerate(order):
+            if step == PASSES_PER_BANK:
                 for i in range(TOKEN_TILES):
                     flip(i, 1)
+            for i in range(TOKEN_TILES):
+                mx_pass(accs[i], i, w, g, 0, N_TILE, step == 0, step == len(order) - 1)
         for i in range(TOKEN_TILES):
             store(accs[i], i, i, 0, N_TILE)
 

@@ -30,7 +30,6 @@ HALVES = PASSES // PASSES_PER_BANK
 QUADRANTS = 4
 PIECES = TOKEN_TILES * (N_TILES - 1 + N_TILE // LAST_N)
 WARM_FIRST = 5
-WARM_BETWEEN = 2
 
 FLOPS = 2 * WEIGHTS * TOKENS * K * N
 
@@ -164,8 +163,6 @@ def tile_myinterleavedmodule_kernel(
         warm(WARM_FIRST)
         for i in range(TOKEN_TILES):
             flip(i, 0)
-            if i % 2 == 1:
-                warm(WARM_BETWEEN)
 
         accs = [psum.tile([P, N_TILE], F32, tag="B", name="acc%d" % i) for i in range(TOKEN_TILES)]
         order = [(w, g) for w in range(WEIGHTS) for g in range(PASSES_PER_BANK)] + [

@@ -45,6 +45,7 @@ def tile_myinterleavedmodule_kernel(
         ctx.enter_context(tc.manual_schedule())
         keep = ctx.enter_context(tc.tile_pool(name="keep", bufs=1))
         stage = ctx.enter_context(tc.tile_pool(name="stage", bufs=4))
+        sorted_pool = ctx.enter_context(tc.tile_pool(name="sorted_pool", bufs=4))
         results = ctx.enter_context(tc.tile_pool(name="results", bufs=PIECES))
         psum = ctx.enter_context(tc.psum_pool(name="psum", bufs=4))
 
@@ -116,17 +117,26 @@ def tile_myinterleavedmodule_kernel(
             for c in range(count):
                 nc.tensor.matmul(idle_bank[:], lhsT=zeros[:, 0:P], rhs=zeros[:], start=True, stop=True)
 
-        def flip(i, h):
+        def sort_words(i, h):
+            x_pairs = x_sb[(i, h)][:].bitcast(F32)
+            in_order = sorted_pool.tile([P, BANK_F32], F32, name="in_order")
+            nc.vector.tensor_copy(
+                out=in_order[:].rearrange("r (s u p) -> r s u p", s=PASSES_PER_BANK, u=PAIRS),
+                in_=x_pairs.rearrange("r (s p u) -> r s u p", s=PASSES_PER_BANK, u=PAIRS),
+            )
+            return in_order
+
+        def flip(i, h, in_order=None):
             x_pairs = x_sb[(i, h)][:].bitcast(F32)
             flipped = psum.tile([P, BANK_F32], F32, tag="A", name="flipped")
             for s in range(PASSES_PER_BANK):
                 for u in range(PAIRS):
                     block = PAIRS * s + u
-                    nc.tensor.transpose(
-                        flipped[:, P * block : P * (block + 1)],
-                        x_pairs[:, PASS_WORDS * s + u : PASS_WORDS * (s + 1) : PAIRS],
-                        ident[:],
-                    )
+                    if in_order is None:
+                        words = x_pairs[:, PASS_WORDS * s + u : PASS_WORDS * (s + 1) : PAIRS]
+                    else:
+                        words = in_order[:, P * block : P * (block + 1)]
+                    nc.tensor.transpose(flipped[:, P * block : P * (block + 1)], words, ident[:])
             grouped = stage.tile([P, PASSES_PER_BANK * P * PACK], BF16, name="grouped", align_bytes=64)
             nc.scalar.copy(
                 out=grouped[:].bitcast(F32).rearrange("p (s r u) -> p s r u", s=PASSES_PER_BANK, u=PAIRS),
@@ -163,6 +173,7 @@ def tile_myinterleavedmodule_kernel(
         warm(WARM_FIRST)
         for i in range(TOKEN_TILES):
             flip(i, 0)
+        second_half = [sort_words(i, 1) for i in range(TOKEN_TILES)]
 
         accs = [psum.tile([P, N_TILE], F32, tag="B", name="acc%d" % i) for i in range(TOKEN_TILES)]
         order = [(w, g) for w in range(WEIGHTS) for g in range(PASSES_PER_BANK)] + [
@@ -171,7 +182,7 @@ def tile_myinterleavedmodule_kernel(
         for step, (w, g) in enumerate(order):
             if step == PASSES_PER_BANK:
                 for i in range(TOKEN_TILES):
-                    flip(i, 1)
+                    flip(i, 1, second_half[i])
             for i in range(TOKEN_TILES):
                 mx_pass(accs[i], i, w, g, 0, N_TILE, step == 0, step == len(order) - 1)
         for i in range(TOKEN_TILES):

@@ -29,6 +29,8 @@ PASSES_PER_BANK = BANK_F32 // (PAIRS * P)
 HALVES = PASSES // PASSES_PER_BANK
 QUADRANTS = 4
 PIECES = TOKEN_TILES * (N_TILES - 1 + N_TILE // LAST_N)
+CODES_PAD = 32
+PLANE_PAD = 64
 WARM_FIRST = 5
 
 FLOPS = 2 * WEIGHTS * TOKENS * K * N
@@ -47,6 +49,7 @@ def tile_myinterleavedmodule_kernel(
         stage = ctx.enter_context(tc.tile_pool(name="stage", bufs=4))
         sorted_pool = ctx.enter_context(tc.tile_pool(name="sorted_pool", bufs=4))
         results = ctx.enter_context(tc.tile_pool(name="results", bufs=PIECES))
+        planes = ctx.enter_context(tc.tile_pool(name="planes", bufs=1))
         psum = ctx.enter_context(tc.psum_pool(name="psum", bufs=4))
 
         ident = keep.tile([P, P], F32, name="ident")
@@ -56,11 +59,11 @@ def tile_myinterleavedmodule_kernel(
             for h in range(HALVES):
                 x_sb[(i, h)] = keep.tile([P, K // HALVES], BF16, name="x_sb%d_%d" % (i, h))
         x_codes = [
-            keep.tile([P, PASSES * P], U32, name="x_codes%d" % i, align_bytes=64)
+            keep.tile([P, CODES_PAD + PASSES * P], U32, name="x_codes%d" % i, align_bytes=256)
             for i in range(TOKEN_TILES)
         ]
         x_scales = [
-            keep.tile([P, PASSES * P], U8, name="x_scales%d" % i, align_bytes=64)
+            planes.tile([P, PASSES * P], U8, name="x_scales%d" % i, align_bytes=256)
             for i in range(TOKEN_TILES)
         ]
         w_chunk = {}
@@ -68,9 +71,11 @@ def tile_myinterleavedmodule_kernel(
             for g in range(PASSES):
                 for j in range(N_TILES):
                     w_chunk[(w, g, j)] = keep.tile(
-                        [P, N_TILE], U32, name="w%d_g%d_j%d" % (w, g, j), align_bytes=64
+                        [P, N_TILE], U32, name="w%d_g%d_j%d" % (w, g, j), align_bytes=256
                     )
-        w_scales = [keep.tile([P, N], U8, name="w_scales%d" % w, align_bytes=64) for w in range(WEIGHTS)]
+        w_scales = [
+            planes.tile([P, PLANE_PAD + N], U8, name="w_scales%d" % w, align_bytes=256) for w in range(WEIGHTS)
+        ]
 
         nc.vector.memset(zeros[:], 0.0)
         for w in range(WEIGHTS):
@@ -84,7 +89,7 @@ def tile_myinterleavedmodule_kernel(
         def load_scales(w, n0, n1):
             for q in range(QUADRANTS):
                 nc.sync.dma_start(
-                    out=w_scales[w][32 * q : 32 * q + 16, n0:n1].bitcast(I32),
+                    out=w_scales[w][32 * q : 32 * q + 16, PLANE_PAD + n0 : PLANE_PAD + n1].bitcast(I32),
                     in_=w_scales_dram[w][:, 4 * q : 4 * q + 4, n0:n1].bitcast(I32),
                 )
 
@@ -144,7 +149,7 @@ def tile_myinterleavedmodule_kernel(
             )
             cols = slice(PASSES_PER_BANK * P * h, PASSES_PER_BANK * P * (h + 1))
             nc.vector.quantize_mx(
-                out=x_codes[i][:, cols].bitcast(FP8X4),
+                out=x_codes[i][:, CODES_PAD + cols.start : CODES_PAD + cols.stop].bitcast(FP8X4),
                 scales=x_scales[i][:, cols],
                 in_=grouped[:],
             )
@@ -154,10 +159,10 @@ def tile_myinterleavedmodule_kernel(
             c0 = n0 % N_TILE
             nc.tensor.matmul_mx(
                 out=acc[:],
-                lhsT=x_codes[i][:, P * g : P * (g + 1)].bitcast(FP8X4),
+                lhsT=x_codes[i][:, CODES_PAD + P * g : CODES_PAD + P * (g + 1)].bitcast(FP8X4),
                 lhsT_scale=x_scales[i][:, P * g : P * (g + 1)],
                 rhs=w_chunk[(w, g, j)][:, c0 : c0 + width].bitcast(FP8X4),
-                rhs_scale=w_scales[w][4 * g : P, n0 : n0 + width],
+                rhs_scale=w_scales[w][4 * g : P, PLANE_PAD + n0 : PLANE_PAD + n0 + width],
                 start=first,
                 stop=last,
             )

@@ -28,10 +28,11 @@ PASS_WORDS = K_PASS // 2
 PASSES_PER_BANK = BANK_F32 // (PAIRS * P)
 HALVES = PASSES // PASSES_PER_BANK
 QUADRANTS = 4
-PIECES = TOKEN_TILES * (N_TILES - 1 + N_TILE // LAST_N)
+PIECES = TOKEN_TILES * (N_TILES - 1 + N_TILE // LAST_N) + 1
 CODES_PAD = 32
 PLANE_PAD = 64
 WARM_FIRST = 5
+WARM_AFTER = [1, 2]
 
 FLOPS = 2 * WEIGHTS * TOKENS * K * N
 
@@ -178,6 +179,8 @@ def tile_myinterleavedmodule_kernel(
         warm(WARM_FIRST)
         for i in range(TOKEN_TILES):
             flip(i, 0)
+            if i in WARM_AFTER:
+                warm(1)
         second_half = [sort_words(i, 1) for i in range(TOKEN_TILES)]
 
         accs = [psum.tile([P, N_TILE], F32, tag="B", name="acc%d" % i) for i in range(TOKEN_TILES)]
@@ -188,8 +191,11 @@ def tile_myinterleavedmodule_kernel(
             if step == PASSES_PER_BANK:
                 for i in range(TOKEN_TILES):
                     flip(i, 1, second_half[i])
-            for i in range(TOKEN_TILES):
+            for i in range(TOKEN_TILES - 1 if step < PASSES_PER_BANK else TOKEN_TILES):
                 mx_pass(accs[i], i, w, g, 0, N_TILE, step == 0, step == len(order) - 1)
+            if step == PASSES_PER_BANK - 1:
+                for s in range(PASSES_PER_BANK):
+                    mx_pass(accs[-1], TOKEN_TILES - 1, order[s][0], order[s][1], 0, N_TILE, s == 0, False)
         for i in range(TOKEN_TILES):
             store(accs[i], i, i, 0, N_TILE)
 
@@ -204,13 +210,13 @@ def tile_myinterleavedmodule_kernel(
             for i in range(TOKEN_TILES):
                 store(accs[i], i, i, N_TILE * j, N_TILE)
 
-        halves = N_TILE // LAST_N
-        for i in range(TOKEN_TILES):
-            for half in range(halves):
-                n0 = N_TILE * (N_TILES - 1) + LAST_N * half
-                piece = halves * i + half
-                acc = psum.tile([P, LAST_N], F32, tag="AB"[piece // 4], name="acc_last")
-                for w in range(WEIGHTS):
-                    for g in range(PASSES):
-                        mx_pass(acc, i, w, g, n0, LAST_N, w == 0 and g == 0, w == WEIGHTS - 1 and g == PASSES - 1)
-                store(acc, piece, i, n0, LAST_N)
+        n0 = N_TILE * (N_TILES - 1)
+        pieces = [(i, n0 + c, LAST_N) for i in range(TOKEN_TILES) for c in range(0, N_TILE, LAST_N)]
+        i, n0, width = pieces[-1]
+        pieces = pieces[:-1] + [(i, n0, width // 2), (i, n0 + width // 2, width // 2)]
+        for piece, (i, n0, width) in enumerate(pieces):
+            acc = psum.tile([P, width], F32, tag="ABA"[piece // 4], name="acc_last")
+            for w in range(WEIGHTS):
+                for g in range(PASSES):
+                    mx_pass(acc, i, w, g, n0, width, w == 0 and g == 0, w == WEIGHTS - 1 and g == PASSES - 1)
+            store(acc, piece, i, n0, width)

@@ -31,7 +31,7 @@ QUADRANTS = 4
 PIECES = TOKEN_TILES * (N_TILES - 1 + N_TILE // LAST_N) + 1
 CODES_PAD = 32
 PLANE_PAD = 64
-WARM_FIRST = 5
+WARM_FIRST = 4
 WARM_AFTER = [1, 2]
 
 FLOPS = 2 * WEIGHTS * TOKENS * K * N
@@ -78,7 +78,7 @@ def tile_myinterleavedmodule_kernel(
             planes.tile([P, PLANE_PAD + N], U8, name="w_scales%d" % w, align_bytes=256) for w in range(WEIGHTS)
         ]
 
-        nc.vector.memset(zeros[:], 0.0)
+        nc.vector.memset(zeros[:].bitcast(I32), 0)
         for w in range(WEIGHTS):
             nc.vector.memset(w_scales[w][:].bitcast(I32), 0)
         make_identity(nc, ident[:])

@@ -104,9 +104,12 @@ def tile_myinterleavedmodule_kernel(
         for w in range(WEIGHTS):
             for i in range(TOKEN_TILES):
                 load_x(i, w)
-            load_scales(w, 0, N_TILE)
+            if w > 0:
+                load_scales(w, 0, N_TILE)
             for g in range(PASSES_PER_BANK):
                 load_chunk(w, g, 0)
+                if w == 0 and g == 0:
+                    load_scales(w, 0, N_TILE)
         for g in range(PASSES_PER_BANK, PASSES):
             for w in range(WEIGHTS):
                 load_chunk(w, g, 0)

from contextlib import ExitStack

import concourse.mybir as mybir
from concourse.masks import make_identity

F32 = mybir.dt.float32
BF16 = mybir.dt.bfloat16
I32 = mybir.dt.int32
U32 = mybir.dt.uint32
U8 = mybir.dt.uint8
FP8X4 = mybir.dt.float8_e4m3fn_x4

P = 128
PACK = 4
K_PASS = P * PACK
TOKENS = 512
K = 2048
N = 2048
PASSES = K // K_PASS
TOKEN_TILES = TOKENS // P
N_TILE = 512
N_TILES = N // N_TILE
LAST_N = 256
WEIGHTS = 2
BANK_F32 = 512
PAIRS = 2
PASS_WORDS = K_PASS // 2
PASSES_PER_BANK = BANK_F32 // (PAIRS * P)
HALVES = PASSES // PASSES_PER_BANK
QUADRANTS = 4
PIECES = TOKEN_TILES * (N_TILES - 1 + N_TILE // LAST_N) + 1
CODES_PAD = 32
PLANE_PAD = 64
WARM_FIRST = 4
WARM_AFTER = [1, 2]

FLOPS = 2 * WEIGHTS * TOKENS * K * N


def tile_myinterleavedmodule_kernel(
    tc, x, W_dense_words, W_dense_scales, W_sparse_words, W_sparse_scales, out
):
    nc = tc.nc
    w_words_dram = [W_dense_words, W_sparse_words]
    w_scales_dram = [W_dense_scales, W_sparse_scales]

    with ExitStack() as ctx:
        ctx.enter_context(tc.manual_schedule())
        keep = ctx.enter_context(tc.tile_pool(name="keep", bufs=1))
        stage = ctx.enter_context(tc.tile_pool(name="stage", bufs=4))
        sorted_pool = ctx.enter_context(tc.tile_pool(name="sorted_pool", bufs=4))
        results = ctx.enter_context(tc.tile_pool(name="results", bufs=PIECES))
        planes = ctx.enter_context(tc.tile_pool(name="planes", bufs=1))
        psum = ctx.enter_context(tc.psum_pool(name="psum", bufs=4))

        ident = keep.tile([P, P], F32, name="ident")
        zeros = keep.tile([P, N_TILE], BF16, name="zeros")
        x_sb = {}
        for i in range(TOKEN_TILES):
            for h in range(HALVES):
                x_sb[(i, h)] = keep.tile([P, K // HALVES], BF16, name="x_sb%d_%d" % (i, h))
        x_codes = [
            keep.tile([P, CODES_PAD + PASSES * P], U32, name="x_codes%d" % i, align_bytes=256)
            for i in range(TOKEN_TILES)
        ]
        x_scales = [
            planes.tile([P, PASSES * P], U8, name="x_scales%d" % i, align_bytes=256)
            for i in range(TOKEN_TILES)
        ]
        w_chunk = {}
        for w in range(WEIGHTS):
            for g in range(PASSES):
                for j in range(N_TILES):
                    w_chunk[(w, g, j)] = keep.tile(
                        [P, N_TILE], U32, name="w%d_g%d_j%d" % (w, g, j), align_bytes=256
                    )
        w_scales = [
            planes.tile([P, PLANE_PAD + N], U8, name="w_scales%d" % w, align_bytes=256) for w in range(WEIGHTS)
        ]

        nc.vector.memset(zeros[:].bitcast(I32), 0)
        for w in range(WEIGHTS):
            nc.vector.memset(w_scales[w][:].bitcast(I32), 0)
        make_identity(nc, ident[:])

        def load_x(i, h):
            width = K // HALVES
            nc.sync.dma_start(out=x_sb[(i, h)][:], in_=x[P * i : P * (i + 1), width * h : width * (h + 1)])

        def load_scales(w, n0, n1):
            for q in range(QUADRANTS):
                nc.sync.dma_start(
                    out=w_scales[w][32 * q : 32 * q + 16, PLANE_PAD + n0 : PLANE_PAD + n1].bitcast(I32),
                    in_=w_scales_dram[w][:, 4 * q : 4 * q + 4, n0:n1].bitcast(I32),
                )

        def load_chunk(w, g, j):
            words = w_words_dram[w][g].rearrange("p n t -> p (n t)")
            nc.sync.dma_start(
                out=w_chunk[(w, g, j)][:].bitcast(I32),
                in_=words[:, PACK * N_TILE * j : PACK * N_TILE * (j + 1)].bitcast(I32),
            )

        for w in range(WEIGHTS):
            for i in range(TOKEN_TILES):
                load_x(i, w)
            if w > 0:
                load_scales(w, 0, N_TILE)
            for g in range(PASSES_PER_BANK):
                load_chunk(w, g, 0)
                if w == 0 and g == 0:
                    load_scales(w, 0, N_TILE)
        for g in range(PASSES_PER_BANK, PASSES):
            for w in range(WEIGHTS):
                load_chunk(w, g, 0)
        for w in range(WEIGHTS):
            load_scales(w, N_TILE, N)
        for j in range(1, N_TILES):
            for w in range(WEIGHTS):
                for g in range(PASSES):
                    load_chunk(w, g, j)

        idle_bank = psum.tile([P, N_TILE], F32, tag="B", name="idle_bank")

        def warm(count):
            for c in range(count):
                nc.tensor.matmul(idle_bank[:], lhsT=zeros[:, 0:P], rhs=zeros[:], start=True, stop=True)

        def sort_words(i, h):
            x_pairs = x_sb[(i, h)][:].bitcast(F32)
            in_order = sorted_pool.tile([P, BANK_F32], F32, name="in_order")
            nc.vector.tensor_copy(
                out=in_order[:].rearrange("r (s u p) -> r s u p", s=PASSES_PER_BANK, u=PAIRS),
                in_=x_pairs.rearrange("r (s p u) -> r s u p", s=PASSES_PER_BANK, u=PAIRS),
            )
            return in_order

        def flip(i, h, in_order=None):
            x_pairs = x_sb[(i, h)][:].bitcast(F32)
            flipped = psum.tile([P, BANK_F32], F32, tag="A", name="flipped")
            for s in range(PASSES_PER_BANK):
                for u in range(PAIRS):
                    block = PAIRS * s + u
                    if in_order is None:
                        words = x_pairs[:, PASS_WORDS * s + u : PASS_WORDS * (s + 1) : PAIRS]
                    else:
                        words = in_order[:, P * block : P * (block + 1)]
                    nc.tensor.transpose(flipped[:, P * block : P * (block + 1)], words, ident[:])
            grouped = stage.tile([P, PASSES_PER_BANK * P * PACK], BF16, name="grouped", align_bytes=64)
            nc.scalar.copy(
                out=grouped[:].bitcast(F32).rearrange("p (s r u) -> p s r u", s=PASSES_PER_BANK, u=PAIRS),
                in_=flipped[:].rearrange("p (s u r) -> p s r u", s=PASSES_PER_BANK, u=PAIRS),
            )
            cols = slice(PASSES_PER_BANK * P * h, PASSES_PER_BANK * P * (h + 1))
            nc.vector.quantize_mx(
                out=x_codes[i][:, CODES_PAD + cols.start : CODES_PAD + cols.stop].bitcast(FP8X4),
                scales=x_scales[i][:, cols],
                in_=grouped[:],
            )

        def mx_pass(acc, i, w, g, n0, width, first, last):
            j = n0 // N_TILE
            c0 = n0 % N_TILE
            nc.tensor.matmul_mx(
                out=acc[:],
                lhsT=x_codes[i][:, CODES_PAD + P * g : CODES_PAD + P * (g + 1)].bitcast(FP8X4),
                lhsT_scale=x_scales[i][:, P * g : P * (g + 1)],
                rhs=w_chunk[(w, g, j)][:, c0 : c0 + width].bitcast(FP8X4),
                rhs_scale=w_scales[w][4 * g : P, PLANE_PAD + n0 : PLANE_PAD + n0 + width],
                start=first,
                stop=last,
            )

        def store(acc, piece, i, n0, width):
            result = results.tile([P, width], F32, name="result")
            if piece % 2 == 0:
                nc.scalar.copy(out=result[:], in_=acc[:])
            else:
                nc.vector.tensor_copy(out=result[:], in_=acc[:])
            nc.sync.dma_start(out=out[P * i : P * (i + 1), n0 : n0 + width], in_=result[:])

        warm(WARM_FIRST)
        for i in range(TOKEN_TILES):
            flip(i, 0)
            if i in WARM_AFTER:
                warm(1)
        second_half = [sort_words(i, 1) for i in range(TOKEN_TILES)]

        accs = [psum.tile([P, N_TILE], F32, tag="B", name="acc%d" % i) for i in range(TOKEN_TILES)]
        order = [(w, g) for w in range(WEIGHTS) for g in range(PASSES_PER_BANK)] + [
            (w, g) for g in range(PASSES_PER_BANK, PASSES) for w in range(WEIGHTS)
        ]
        for step, (w, g) in enumerate(order):
            if step == PASSES_PER_BANK:
                for i in range(TOKEN_TILES):
                    flip(i, 1, second_half[i])
            for i in range(TOKEN_TILES - 1 if step < PASSES_PER_BANK else TOKEN_TILES):
                mx_pass(accs[i], i, w, g, 0, N_TILE, step == 0, step == len(order) - 1)
            if step == PASSES_PER_BANK - 1:
                for s in range(PASSES_PER_BANK):
                    mx_pass(accs[-1], TOKEN_TILES - 1, order[s][0], order[s][1], 0, N_TILE, s == 0, False)
        for i in range(TOKEN_TILES):
            store(accs[i], i, i, 0, N_TILE)

        for j in range(1, N_TILES - 1):
            accs = [
                psum.tile([P, N_TILE], F32, tag="AB"[(j + 1) % 2], name="acc%d" % i) for i in range(TOKEN_TILES)
            ]
            for w in range(WEIGHTS):
                for g in range(PASSES):
                    for i in range(TOKEN_TILES):
                        mx_pass(accs[i], i, w, g, N_TILE * j, N_TILE, w == 0 and g == 0, w == WEIGHTS - 1 and g == PASSES - 1)
            for i in range(TOKEN_TILES):
                store(accs[i], i, i, N_TILE * j, N_TILE)

        n0 = N_TILE * (N_TILES - 1)
        pieces = [(i, n0 + c, LAST_N) for i in range(TOKEN_TILES) for c in range(0, N_TILE, LAST_N)]
        i, n0, width = pieces[-1]
        pieces = pieces[:-1] + [(i, n0, width // 2), (i, n0 + width // 2, width // 2)]
        for piece, (i, n0, width) in enumerate(pieces):
            acc = psum.tile([P, width], F32, tag="ABA"[piece // 4], name="acc_last")
            for w in range(WEIGHTS):
                for g in range(PASSES):
                    mx_pass(acc, i, w, g, n0, width, w == 0 and g == 0, w == WEIGHTS - 1 and g == PASSES - 1)
            store(acc, piece, i, n0, width)
